import numpy as np
import ml_dtypes


def mxq(x, axis, fmt="e4m3"):
    dtype, down = {"e4m3": (ml_dtypes.float8_e4m3fn, 7), "e5m2": (ml_dtypes.float8_e5m2, 14)}[fmt]
    v = np.moveaxis(np.asarray(x, np.float32).astype(ml_dtypes.bfloat16).astype(np.float64), axis, -1)
    blocks = v.reshape(v.shape[:-1] + (-1, 32))
    amax = np.abs(blocks).max(-1, keepdims=True)
    byte = np.maximum(np.where(amax > 0, np.frexp(amax)[1] - 1 + 127, 0) - down, 1)
    scale = np.exp2(byte - 127.0)
    codes = (blocks / scale).astype(np.float32).astype(dtype).astype(np.float64)
    return np.moveaxis((codes * scale).reshape(v.shape), -1, axis)


WIDE = False


def mx_kscale(k):
    if not WIDE:
        return np.ones(k)
    levels = np.array([10, -10, 5, -5, 0])
    if k % 512:
        return np.exp2(np.random.permutation(np.resize(levels, k // 32))).repeat(32)
    a = np.empty((k // 512, 16))
    for p in range(k // 512):
        a[p, :8] = np.random.permutation(np.resize(levels, 8))
        for g in range(8):
            far = levels[np.abs(levels - a[p, g]) >= 10]
            a[p, g + 8] = far[np.random.randint(len(far))]
    return np.exp2(a.ravel()).repeat(32)


BF16 = ml_dtypes.bfloat16


def bf(x):
    return np.asarray(x, np.float32).astype(BF16)


def f64(x):
    return np.asarray(x).astype(np.float64)


N, MI, MO, LMAX = 128, 512, 128, 3
C = (LMAX + 1) ** 2


def setup_inputs():
    s = mx_kscale(MI)
    d = {"x": bf(np.random.standard_normal((N, MI, C)) * s[None, :, None])}
    for l in range(LMAX + 1):
        d["w%d" % l] = bf(np.random.standard_normal((MI, MO)) / np.sqrt(MI) / s[:, None])
    return d


def reference(x, w0, w1, w2, w3):
    xq = mxq(f64(x), 1, "e4m3")
    parts = []
    for l, w in enumerate([w0, w1, w2, w3]):
        xl = xq[:, :, l * l:(l + 1) ** 2].transpose(0, 2, 1)
        parts.append((xl @ mxq(f64(w), 0, "e4m3")).transpose(0, 2, 1))
    return np.concatenate(parts, axis=2)

@@ -1,0 +1,116 @@
+from contextlib import ExitStack
+
+import concourse.mybir as mybir
+from concourse.masks import make_identity
+
+BF16 = mybir.dt.bfloat16
+F32 = mybir.dt.float32
+U32 = mybir.dt.uint32
+U8 = mybir.dt.uint8
+FP8X4 = mybir.dt.float8_e4m3fn_x4
+
+P = 128
+PACK = 4
+N, MI, MO, LMAX = 128, 512, 128, 3
+C = (LMAX + 1) ** 2
+DEGREES = LMAX + 1
+LOADS = 8
+I_LOAD = MI // LOADS
+GROUP = 4
+GROUPS = C // GROUP
+PAIR = 2
+
+FLOPS = 2 * N * MI * MO * C
+
+
+def tile_irrepsstridelinear_s_kernel(tc, x, w0, w1, w2, w3, out):
+    nc = tc.nc
+    weights = [w0, w1, w2, w3]
+    degree_of_channel = [l for l in range(DEGREES) for m in range(2 * l + 1)]
+
+    with ExitStack() as ctx:
+        keep = ctx.enter_context(tc.tile_pool(name="keep", bufs=1))
+        psum_t = ctx.enter_context(tc.psum_pool(name="psum_t", bufs=4))
+        psum_o = ctx.enter_context(tc.psum_pool(name="psum_o", bufs=4))
+
+        identity = keep.tile([P, P], F32)
+        make_identity(nc, identity[:])
+
+        x_raw = keep.tile([P, MI, C], BF16)
+        for q in range(LOADS):
+            nc.sync.dma_start(
+                out=x_raw[:, q * I_LOAD : (q + 1) * I_LOAD, :].rearrange("p i c -> p (i c)"),
+                in_=x[:, q * I_LOAD : (q + 1) * I_LOAD, :].rearrange("n i c -> n (i c)"),
+            )
+        w_raw = keep.tile([P, DEGREES, PACK, MO], BF16)
+        for l in range(DEGREES):
+            nc.sync.dma_start(
+                out=w_raw[:, l, :, :].rearrange("p t o -> p (t o)"),
+                in_=weights[l].rearrange("(p t) o -> p (t o)", t=PACK),
+            )
+
+        x_by_channel = keep.tile([P, C, MI], BF16)
+        x_grouped = keep.tile([P, C, N * PACK], BF16, align_bytes=64)
+        for q in range(LOADS):
+            i_range = slice(q * I_LOAD, (q + 1) * I_LOAD)
+            nc.vector.tensor_copy(
+                out=x_by_channel[:, :, i_range].rearrange("p (a b) i -> p a i b", b=4),
+                in_=x_raw[:, i_range, :].rearrange("p i (a b) -> p a i b", b=4),
+            )
+        words = x_by_channel[:].bitcast(F32)
+        x_grouped_words = x_grouped[:].bitcast(F32)
+        for a in range(C // PAIR):
+            flipped = psum_t.tile([P, PAIR, 2, N], F32)
+            for b in range(PAIR):
+                for u in range(2):
+                    nc.tensor.transpose(flipped[:, b, u, :], words[:, a * PAIR + b, u::2], identity[:])
+            nc.scalar.copy(
+                out=x_grouped_words[:, a * PAIR : (a + 1) * PAIR, :].rearrange("p b (n u) -> p b n u", u=2),
+                in_=flipped[:].rearrange("p b u n -> p b n u"),
+            )
+
+        w_grouped = keep.tile([P, DEGREES, MO, PACK], BF16, align_bytes=64)
+        for l in range(DEGREES):
+            nc.vector.tensor_copy(
+                out=w_grouped[:, l, :, :].rearrange("p (a b) t -> p a t b", b=4),
+                in_=w_raw[:, l, :, :].rearrange("p t (a b) -> p a t b", b=4),
+            )
+        w_codes = keep.tile([P, DEGREES * MO], U32, align_bytes=64)
+        w_scales = keep.tile([P, DEGREES * MO], U8, align_bytes=64)
+        nc.vector.quantize_mx(
+            out=w_codes[:].bitcast(FP8X4),
+            scales=w_scales[:],
+            in_=w_grouped[:].rearrange("p l o t -> p (l o t)"),
+        )
+
+        x_codes = keep.tile([P, C * N], U32, align_bytes=64)
+        x_scales = keep.tile([P, C * N], U8, align_bytes=64)
+        result = keep.tile([P, MO, C], F32)
+        for a in range(GROUPS):
+            columns = slice(a * GROUP * N, (a + 1) * GROUP * N)
+            nc.vector.quantize_mx(
+                out=x_codes[:, columns].bitcast(FP8X4),
+                scales=x_scales[:, columns],
+                in_=x_grouped[:, a * GROUP : (a + 1) * GROUP, :].rearrange("p c m -> p (c m)"),
+            )
+            acc = psum_o.tile([P, GROUP, MO], F32)
+            for b in range(GROUP):
+                c = a * GROUP + b
+                l = degree_of_channel[c]
+                nc.tensor.matmul_mx(
+                    out=acc[:, b, :],
+                    lhsT=x_codes[:, c * N : (c + 1) * N].bitcast(FP8X4),
+                    lhsT_scale=x_scales[:, c * N : (c + 1) * N],
+                    rhs=w_codes[:, l * MO : (l + 1) * MO].bitcast(FP8X4),
+                    rhs_scale=w_scales[:, l * MO : (l + 1) * MO],
+                    start=True,
+                    stop=True,
+                )
+            nc.scalar.copy(
+                out=result[:, :, a * GROUP : (a + 1) * GROUP],
+                in_=acc[:].rearrange("p b o -> p o b"),
+            )
+        nc.sync.dma_start(
+            out=out.rearrange("n o c -> n (o c)"),
+            in_=result[:].rearrange("p o c -> p (o c)"),
+        )

@@ -20,6 +20,8 @@ GROUP = 4
 GROUPS = C // GROUP
 PAIR = 2
 
+VECTOR_PAIRS = [3, 6]
+
 FLOPS = 2 * N * MI * MO * C
 
 
@@ -49,31 +51,21 @@ def tile_irrepsstridelinear_s_kernel(tc, x, w0, w1, w2, w3, out):
                 in_=weights[l].rearrange("(p t) o -> p (t o)", t=PACK),
             )
 
-        x_by_channel = keep.tile([P, C, MI], BF16)
-        x_grouped = keep.tile([P, C, N * PACK], BF16, align_bytes=64)
+        x_by_channel = keep.tile([P, C, 2, MI // 2], BF16)
         for q in range(LOADS):
             i_range = slice(q * I_LOAD, (q + 1) * I_LOAD)
-            nc.vector.tensor_copy(
-                out=x_by_channel[:, :, i_range].rearrange("p (a b) i -> p a i b", b=4),
-                in_=x_raw[:, i_range, :].rearrange("p i (a b) -> p a i b", b=4),
-            )
-        words = x_by_channel[:].bitcast(F32)
-        x_grouped_words = x_grouped[:].bitcast(F32)
-        for a in range(C // PAIR):
-            flipped = psum_t.tile([P, PAIR, 2, N], F32)
-            for b in range(PAIR):
-                for u in range(2):
-                    nc.tensor.transpose(flipped[:, b, u, :], words[:, a * PAIR + b, u::2], identity[:])
-            nc.scalar.copy(
-                out=x_grouped_words[:, a * PAIR : (a + 1) * PAIR, :].rearrange("p b (n u) -> p b n u", u=2),
-                in_=flipped[:].rearrange("p b u n -> p b n u"),
-            )
+            k_range = slice(q * I_LOAD // 2, (q + 1) * I_LOAD // 2)
+            for a in [slice(0, 4)] if q < LOADS - 1 else [slice(a, a + 1) for a in range(4)]:
+                nc.vector.tensor_copy(
+                    out=x_by_channel[:, :, :, k_range].rearrange("p (a b) u k -> p a u k b", b=4)[:, a],
+                    in_=x_raw[:, i_range, :].rearrange("p (k u) (a b) -> p a u k b", u=2, b=4)[:, a],
+                )
 
         w_grouped = keep.tile([P, DEGREES, MO, PACK], BF16, align_bytes=64)
         for l in range(DEGREES):
             nc.vector.tensor_copy(
-                out=w_grouped[:, l, :, :].rearrange("p (a b) t -> p a t b", b=4),
-                in_=w_raw[:, l, :, :].rearrange("p t (a b) -> p a t b", b=4),
+                out=w_grouped[:, l, :, :].rearrange("p (a b) (u e) -> p a u e b", b=4, u=2),
+                in_=w_raw[:, l, :, :].rearrange("p (e u) (a b) -> p a u e b", b=4, u=2),
             )
         w_codes = keep.tile([P, DEGREES * MO], U32, align_bytes=64)
         w_scales = keep.tile([P, DEGREES * MO], U8, align_bytes=64)
@@ -83,34 +75,84 @@ def tile_irrepsstridelinear_s_kernel(tc, x, w0, w1, w2, w3, out):
             in_=w_grouped[:].rearrange("p l o t -> p (l o t)"),
         )
 
+        x_grouped = keep.tile([P, C, N * PACK], BF16, align_bytes=64)
+        words = x_by_channel[:].bitcast(F32)
+        x_grouped_words = x_grouped[:].bitcast(F32)
         x_codes = keep.tile([P, C * N], U32, align_bytes=64)
         x_scales = keep.tile([P, C * N], U8, align_bytes=64)
         result = keep.tile([P, MO, C], F32)
-        for a in range(GROUPS):
-            columns = slice(a * GROUP * N, (a + 1) * GROUP * N)
+
+        def transpose_pair(a):
+            flipped = psum_t.tile([P, PAIR, 2, N], F32)
+            for b in range(PAIR):
+                for u in range(2):
+                    nc.tensor.transpose(flipped[:, b, u, :], words[:, a * PAIR + b, u, :], identity[:])
+            return flipped
+
+        def collect(engine_copy, a, flipped):
+            engine_copy(
+                out=x_grouped_words[:, a * PAIR : (a + 1) * PAIR, :].rearrange("p b (n u) -> p b n u", u=2),
+                in_=flipped[:].rearrange("p b u n -> p b n u"),
+            )
+
+        def quantise(c_range):
+            columns = slice(c_range.start * N, c_range.stop * N)
             nc.vector.quantize_mx(
                 out=x_codes[:, columns].bitcast(FP8X4),
                 scales=x_scales[:, columns],
-                in_=x_grouped[:, a * GROUP : (a + 1) * GROUP, :].rearrange("p c m -> p (c m)"),
+                in_=x_grouped[:, c_range, :].rearrange("p c m -> p (c m)"),
             )
-            acc = psum_o.tile([P, GROUP, MO], F32)
+
+        def multiply(g, o_range):
+            width = o_range.stop - o_range.start
+            acc = psum_o.tile([P, GROUP, width], F32)
             for b in range(GROUP):
-                c = a * GROUP + b
-                l = degree_of_channel[c]
+                c = g * GROUP + b
+                w_columns = slice(
+                    degree_of_channel[c] * MO + o_range.start, degree_of_channel[c] * MO + o_range.stop
+                )
                 nc.tensor.matmul_mx(
                     out=acc[:, b, :],
                     lhsT=x_codes[:, c * N : (c + 1) * N].bitcast(FP8X4),
                     lhsT_scale=x_scales[:, c * N : (c + 1) * N],
-                    rhs=w_codes[:, l * MO : (l + 1) * MO].bitcast(FP8X4),
-                    rhs_scale=w_scales[:, l * MO : (l + 1) * MO],
+                    rhs=w_codes[:, w_columns].bitcast(FP8X4),
+                    rhs_scale=w_scales[:, w_columns],
                     start=True,
                     stop=True,
                 )
-            nc.scalar.copy(
-                out=result[:, :, a * GROUP : (a + 1) * GROUP],
+            return acc
+
+        def gather(engine_copy, g, o_range, acc):
+            engine_copy(
+                out=result[:, o_range, g * GROUP : (g + 1) * GROUP],
                 in_=acc[:].rearrange("p b o -> p o b"),
             )
-        nc.sync.dma_start(
-            out=out.rearrange("n o c -> n (o c)"),
-            in_=result[:].rearrange("p o c -> p (o c)"),
-        )
+
+        all_o = slice(0, MO)
+        copy_of_pair = [nc.scalar.copy] * (C // PAIR)
+        for a in VECTOR_PAIRS:
+            copy_of_pair[a] = nc.vector.tensor_copy
+        with tc.manual_schedule():
+            for a in range(C // PAIR):
+                collect(copy_of_pair[a], a, transpose_pair(a))
+                if a == 2:
+                    quantise(slice(0, 4))
+                if a == 4:
+                    quantise(slice(4, 8))
+                if a == 5:
+                    gather(nc.scalar.copy, 0, all_o, multiply(0, all_o))
+                if a == 6:
+                    quantise(slice(8, 12))
+                    quantise(slice(12, 14))
+            gather(nc.scalar.copy, 1, all_o, multiply(1, all_o))
+            quantise(slice(14, 16))
+            gather(nc.vector.tensor_copy, 2, all_o, multiply(2, all_o))
+            low, high = slice(0, MO // 2), slice(MO // 2, MO)
+            acc_low, acc_high = multiply(3, low), multiply(3, high)
+            gather(nc.vector.tensor_copy, 3, low, acc_low)
+            gather(nc.scalar.copy, 3, high, acc_high)
+            for o_range in [low, high]:
+                nc.sync.dma_start(
+                    out=out[:, o_range, :].rearrange("n o c -> n (o c)"),
+                    in_=result[:, o_range, :].rearrange("p o c -> p (o c)"),
+                )

@@ -22,6 +22,9 @@ PAIR = 2
 
 VECTOR_PAIRS = [3, 6]
 
+WARM = 4
+WARM_PAIRS = [1, 4]
+
 FLOPS = 2 * N * MI * MO * C
 
 
@@ -49,6 +52,15 @@ def tile_irrepsstridelinear_s_kernel(tc, x, w0, w1, w2, w3, out):
             nc.sync.dma_start(
                 out=w_raw[:, l, :, :].rearrange("p t o -> p (t o)"),
                 in_=weights[l].rearrange("(p t) o -> p (t o)", t=PACK),
+            )
+
+        x_words = x_raw[:].rearrange("p i c -> p (i c)").bitcast(F32)
+        dummy = psum_o.tile([P, GROUP, MO], F32, name="acc")
+
+        def warm(q):
+            first = q * I_LOAD * C // 2
+            nc.tensor.matmul(
+                dummy[:, 0, :], lhsT=identity[:], rhs=x_words[:, first : first + P], start=True, stop=True
             )
 
         x_by_channel = keep.tile([P, C, 2, MI // 2], BF16)
@@ -133,8 +145,12 @@ def tile_irrepsstridelinear_s_kernel(tc, x, w0, w1, w2, w3, out):
         for a in VECTOR_PAIRS:
             copy_of_pair[a] = nc.vector.tensor_copy
         with tc.manual_schedule():
+            for q in range(LOADS - WARM, LOADS):
+                warm(q)
             for a in range(C // PAIR):
                 collect(copy_of_pair[a], a, transpose_pair(a))
+                if a in WARM_PAIRS:
+                    warm(LOADS - 1)
                 if a == 2:
                     quantise(slice(0, 4))
                 if a == 4:

@@ -20,9 +20,9 @@ GROUP = 4
 GROUPS = C // GROUP
 PAIR = 2
 
-VECTOR_PAIRS = [3, 6]
+VECTOR_PAIRS = [2]
 
-WARM = 4
+WARM = range(3, 7)
 WARM_PAIRS = [1, 4]
 
 FLOPS = 2 * N * MI * MO * C
@@ -35,8 +35,7 @@ def tile_irrepsstridelinear_s_kernel(tc, x, w0, w1, w2, w3, out):
 
     with ExitStack() as ctx:
         keep = ctx.enter_context(tc.tile_pool(name="keep", bufs=1))
-        psum_t = ctx.enter_context(tc.psum_pool(name="psum_t", bufs=4))
-        psum_o = ctx.enter_context(tc.psum_pool(name="psum_o", bufs=4))
+        psum = ctx.enter_context(tc.psum_pool(name="psum", bufs=8))
 
         identity = keep.tile([P, P], F32)
         make_identity(nc, identity[:])
@@ -55,7 +54,7 @@ def tile_irrepsstridelinear_s_kernel(tc, x, w0, w1, w2, w3, out):
             )
 
         x_words = x_raw[:].rearrange("p i c -> p (i c)").bitcast(F32)
-        dummy = psum_o.tile([P, GROUP, MO], F32, name="acc")
+        dummy = psum.tile([P, GROUP, MO], F32, name="bank")
 
         def warm(q):
             first = q * I_LOAD * C // 2
@@ -95,7 +94,7 @@ def tile_irrepsstridelinear_s_kernel(tc, x, w0, w1, w2, w3, out):
         result = keep.tile([P, MO, C], F32)
 
         def transpose_pair(a):
-            flipped = psum_t.tile([P, PAIR, 2, N], F32)
+            flipped = psum.tile([P, PAIR, 2, N], F32, name="bank")
             for b in range(PAIR):
                 for u in range(2):
                     nc.tensor.transpose(flipped[:, b, u, :], words[:, a * PAIR + b, u, :], identity[:])
@@ -115,20 +114,17 @@ def tile_irrepsstridelinear_s_kernel(tc, x, w0, w1, w2, w3, out):
                 in_=x_grouped[:, c_range, :].rearrange("p c m -> p (c m)"),
             )
 
-        def multiply(g, o_range):
-            width = o_range.stop - o_range.start
-            acc = psum_o.tile([P, GROUP, width], F32)
+        def multiply(g):
+            acc = psum.tile([P, GROUP, MO], F32, name="bank")
             for b in range(GROUP):
                 c = g * GROUP + b
-                w_columns = slice(
-                    degree_of_channel[c] * MO + o_range.start, degree_of_channel[c] * MO + o_range.stop
-                )
+                l = degree_of_channel[c]
                 nc.tensor.matmul_mx(
                     out=acc[:, b, :],
                     lhsT=x_codes[:, c * N : (c + 1) * N].bitcast(FP8X4),
                     lhsT_scale=x_scales[:, c * N : (c + 1) * N],
-                    rhs=w_codes[:, w_columns].bitcast(FP8X4),
-                    rhs_scale=w_scales[:, w_columns],
+                    rhs=w_codes[:, l * MO : (l + 1) * MO].bitcast(FP8X4),
+                    rhs_scale=w_scales[:, l * MO : (l + 1) * MO],
                     start=True,
                     stop=True,
                 )
@@ -137,37 +133,29 @@ def tile_irrepsstridelinear_s_kernel(tc, x, w0, w1, w2, w3, out):
         def gather(engine_copy, g, o_range, acc):
             engine_copy(
                 out=result[:, o_range, g * GROUP : (g + 1) * GROUP],
-                in_=acc[:].rearrange("p b o -> p o b"),
+                in_=acc[:, :, o_range].rearrange("p b o -> p o b"),
             )
 
-        all_o = slice(0, MO)
         copy_of_pair = [nc.scalar.copy] * (C // PAIR)
         for a in VECTOR_PAIRS:
             copy_of_pair[a] = nc.vector.tensor_copy
+        copy_of_group = [nc.scalar.copy, nc.scalar.copy, nc.scalar.copy, nc.vector.tensor_copy]
         with tc.manual_schedule():
-            for q in range(LOADS - WARM, LOADS):
+            for q in WARM:
                 warm(q)
             for a in range(C // PAIR):
                 collect(copy_of_pair[a], a, transpose_pair(a))
                 if a in WARM_PAIRS:
                     warm(LOADS - 1)
-                if a == 2:
-                    quantise(slice(0, 4))
-                if a == 4:
-                    quantise(slice(4, 8))
-                if a == 5:
-                    gather(nc.scalar.copy, 0, all_o, multiply(0, all_o))
-                if a == 6:
-                    quantise(slice(8, 12))
-                    quantise(slice(12, 14))
-            gather(nc.scalar.copy, 1, all_o, multiply(1, all_o))
-            quantise(slice(14, 16))
-            gather(nc.vector.tensor_copy, 2, all_o, multiply(2, all_o))
-            low, high = slice(0, MO // 2), slice(MO // 2, MO)
-            acc_low, acc_high = multiply(3, low), multiply(3, high)
-            gather(nc.vector.tensor_copy, 3, low, acc_low)
-            gather(nc.scalar.copy, 3, high, acc_high)
-            for o_range in [low, high]:
+                if a in (2, 3, 5):
+                    g = a // 2 if a > 2 else 0
+                    quantise(slice(g * GROUP, (g + 1) * GROUP))
+                if a in (6, 7):
+                    quantise(slice(2 * a, 2 * a + 2))
+            acc = [multiply(g) for g in range(GROUPS)]
+            for o_range in [slice(0, MO // 2), slice(MO // 2, MO)]:
+                for g in range(GROUPS):
+                    gather(copy_of_group[g], g, o_range, acc[g])
                 nc.sync.dma_start(
                     out=out[:, o_range, :].rearrange("n o c -> n (o c)"),
                     in_=result[:, o_range, :].rearrange("p o c -> p (o c)"),

@@ -18,12 +18,13 @@ LOADS = 8
 I_LOAD = MI // LOADS
 GROUP = 4
 GROUPS = C // GROUP
-PAIR = 2
 
-VECTOR_PAIRS = [2]
+STORES = [32, 96]
+BANKS = [1, 1, 2, 2, 2, 2, 2, 2, 2]
+VECTOR_BANKS = [1, 3]
 
 WARM = range(3, 7)
-WARM_PAIRS = [1, 4]
+WARM_BANKS = [4, 6]
 
 FLOPS = 2 * N * MI * MO * C
 
@@ -74,17 +75,19 @@ def tile_irrepsstridelinear_s_kernel(tc, x, w0, w1, w2, w3, out):
 
         w_grouped = keep.tile([P, DEGREES, MO, PACK], BF16, align_bytes=64)
         for l in range(DEGREES):
-            nc.vector.tensor_copy(
+            (nc.scalar.copy if l == 0 else nc.vector.tensor_copy)(
                 out=w_grouped[:, l, :, :].rearrange("p (a b) (u e) -> p a u e b", b=4, u=2),
                 in_=w_raw[:, l, :, :].rearrange("p (e u) (a b) -> p a u e b", b=4, u=2),
             )
         w_codes = keep.tile([P, DEGREES * MO], U32, align_bytes=64)
         w_scales = keep.tile([P, DEGREES * MO], U8, align_bytes=64)
-        nc.vector.quantize_mx(
-            out=w_codes[:].bitcast(FP8X4),
-            scales=w_scales[:],
-            in_=w_grouped[:].rearrange("p l o t -> p (l o t)"),
-        )
+
+        def quantise_weights():
+            nc.vector.quantize_mx(
+                out=w_codes[:].bitcast(FP8X4),
+                scales=w_scales[:],
+                in_=w_grouped[:].rearrange("p l o t -> p (l o t)"),
+            )
 
         x_grouped = keep.tile([P, C, N * PACK], BF16, align_bytes=64)
         words = x_by_channel[:].bitcast(F32)
@@ -93,16 +96,16 @@ def tile_irrepsstridelinear_s_kernel(tc, x, w0, w1, w2, w3, out):
         x_scales = keep.tile([P, C * N], U8, align_bytes=64)
         result = keep.tile([P, MO, C], F32)
 
-        def transpose_pair(a):
-            flipped = psum.tile([P, PAIR, 2, N], F32, name="bank")
-            for b in range(PAIR):
+        def transpose(c_range):
+            flipped = psum.tile([P, len(c_range), 2, N], F32, name="bank")
+            for b, c in enumerate(c_range):
                 for u in range(2):
-                    nc.tensor.transpose(flipped[:, b, u, :], words[:, a * PAIR + b, u, :], identity[:])
+                    nc.tensor.transpose(flipped[:, b, u, :], words[:, c, u, :], identity[:])
             return flipped
 
-        def collect(engine_copy, a, flipped):
+        def collect(engine_copy, c_range, flipped):
             engine_copy(
-                out=x_grouped_words[:, a * PAIR : (a + 1) * PAIR, :].rearrange("p b (n u) -> p b n u", u=2),
+                out=x_grouped_words[:, c_range.start : c_range.stop, :].rearrange("p b (n u) -> p b n u", u=2),
                 in_=flipped[:].rearrange("p b u n -> p b n u"),
             )
 
@@ -111,7 +114,7 @@ def tile_irrepsstridelinear_s_kernel(tc, x, w0, w1, w2, w3, out):
             nc.vector.quantize_mx(
                 out=x_codes[:, columns].bitcast(FP8X4),
                 scales=x_scales[:, columns],
-                in_=x_grouped[:, c_range, :].rearrange("p c m -> p (c m)"),
+                in_=x_grouped[:, c_range.start : c_range.stop, :].rearrange("p c m -> p (c m)"),
             )
 
         def multiply(g):
@@ -136,27 +139,43 @@ def tile_irrepsstridelinear_s_kernel(tc, x, w0, w1, w2, w3, out):
                 in_=acc[:, :, o_range].rearrange("p b o -> p o b"),
             )
 
-        copy_of_pair = [nc.scalar.copy] * (C // PAIR)
-        for a in VECTOR_PAIRS:
-            copy_of_pair[a] = nc.vector.tensor_copy
-        copy_of_group = [nc.scalar.copy, nc.scalar.copy, nc.scalar.copy, nc.vector.tensor_copy]
         with tc.manual_schedule():
             for q in WARM:
                 warm(q)
-            for a in range(C // PAIR):
-                collect(copy_of_pair[a], a, transpose_pair(a))
-                if a in WARM_PAIRS:
+            for_vector = []
+            for i, count in enumerate(BANKS):
+                c_range = range(sum(BANKS[:i]), sum(BANKS[:i]) + count)
+                flipped = transpose(c_range)
+                if i in VECTOR_BANKS:
+                    for_vector.append((c_range, flipped))
+                else:
+                    collect(nc.scalar.copy, c_range, flipped)
+                if i in WARM_BANKS:
                     warm(LOADS - 1)
-                if a in (2, 3, 5):
-                    g = a // 2 if a > 2 else 0
-                    quantise(slice(g * GROUP, (g + 1) * GROUP))
-                if a in (6, 7):
-                    quantise(slice(2 * a, 2 * a + 2))
+            collect(nc.vector.tensor_copy, *for_vector[0])
+            quantise_weights()
+            collect(nc.vector.tensor_copy, *for_vector[1])
+            quantise(range(0, 4))
+            quantise(range(4, 8))
+            quantise(range(8, 12))
+            quantise(range(12, 14))
+            quantise(range(14, 16))
             acc = [multiply(g) for g in range(GROUPS)]
-            for o_range in [slice(0, MO // 2), slice(MO // 2, MO)]:
-                for g in range(GROUPS):
-                    gather(copy_of_group[g], g, o_range, acc[g])
+            low, high = slice(0, STORES[0]), slice(STORES[0], MO)
+
+            def store(o_range):
                 nc.sync.dma_start(
                     out=out[:, o_range, :].rearrange("n o c -> n (o c)"),
                     in_=result[:, o_range, :].rearrange("p o c -> p (o c)"),
                 )
+
+            gather(nc.scalar.copy, 0, low, acc[0])
+            gather(nc.scalar.copy, 1, low, acc[1])
+            gather(nc.scalar.copy, 0, high, acc[0])
+            gather(nc.scalar.copy, 2, low, acc[2])
+            gather(nc.vector.tensor_copy, 3, low, acc[3])
+            store(low)
+            gather(nc.scalar.copy, 1, high, acc[1])
+            gather(nc.scalar.copy, 2, high, acc[2])
+            gather(nc.vector.tensor_copy, 3, high, acc[3])
+            store(high)

@@ -21,7 +21,7 @@ GROUPS = C // GROUP
 
 STORES = [32, 96]
 BANKS = [1, 1, 2, 2, 2, 2, 2, 2, 2]
-VECTOR_BANKS = [1, 3]
+VECTOR_BANKS = [3]
 
 WARM = range(3, 7)
 WARM_BANKS = [4, 6]
@@ -82,11 +82,12 @@ def tile_irrepsstridelinear_s_kernel(tc, x, w0, w1, w2, w3, out):
         w_codes = keep.tile([P, DEGREES * MO], U32, align_bytes=64)
         w_scales = keep.tile([P, DEGREES * MO], U8, align_bytes=64)
 
-        def quantise_weights():
+        def quantise_weights(degrees):
+            columns = slice(degrees.start * MO, degrees.stop * MO)
             nc.vector.quantize_mx(
-                out=w_codes[:].bitcast(FP8X4),
-                scales=w_scales[:],
-                in_=w_grouped[:].rearrange("p l o t -> p (l o t)"),
+                out=w_codes[:, columns].bitcast(FP8X4),
+                scales=w_scales[:, columns],
+                in_=w_grouped[:, degrees.start : degrees.stop].rearrange("p l o t -> p (l o t)"),
             )
 
         x_grouped = keep.tile([P, C, N * PACK], BF16, align_bytes=64)
@@ -152,9 +153,9 @@ def tile_irrepsstridelinear_s_kernel(tc, x, w0, w1, w2, w3, out):
                     collect(nc.scalar.copy, c_range, flipped)
                 if i in WARM_BANKS:
                     warm(LOADS - 1)
+            quantise_weights(range(0, 2))
+            quantise_weights(range(2, 4))
             collect(nc.vector.tensor_copy, *for_vector[0])
-            quantise_weights()
-            collect(nc.vector.tensor_copy, *for_vector[1])
             quantise(range(0, 4))
             quantise(range(4, 8))
             quantise(range(8, 12))

from contextlib import ExitStack

import concourse.mybir as mybir
from concourse.masks import make_identity

BF16 = mybir.dt.bfloat16
F32 = mybir.dt.float32
U32 = mybir.dt.uint32
U8 = mybir.dt.uint8
FP8X4 = mybir.dt.float8_e4m3fn_x4

P = 128
PACK = 4
N, MI, MO, LMAX = 128, 512, 128, 3
C = (LMAX + 1) ** 2
DEGREES = LMAX + 1
LOADS = 8
I_LOAD = MI // LOADS
GROUP = 4
GROUPS = C // GROUP

STORES = [32, 96]
BANKS = [1, 1, 2, 2, 2, 2, 2, 2, 2]
VECTOR_BANKS = [3]

WARM = range(3, 7)
WARM_BANKS = [4, 6]

FLOPS = 2 * N * MI * MO * C


def tile_irrepsstridelinear_s_kernel(tc, x, w0, w1, w2, w3, out):
    nc = tc.nc
    weights = [w0, w1, w2, w3]
    degree_of_channel = [l for l in range(DEGREES) for m in range(2 * l + 1)]

    with ExitStack() as ctx:
        keep = ctx.enter_context(tc.tile_pool(name="keep", bufs=1))
        psum = ctx.enter_context(tc.psum_pool(name="psum", bufs=8))

        identity = keep.tile([P, P], F32)
        make_identity(nc, identity[:])

        x_raw = keep.tile([P, MI, C], BF16)
        for q in range(LOADS):
            nc.sync.dma_start(
                out=x_raw[:, q * I_LOAD : (q + 1) * I_LOAD, :].rearrange("p i c -> p (i c)"),
                in_=x[:, q * I_LOAD : (q + 1) * I_LOAD, :].rearrange("n i c -> n (i c)"),
            )
        w_raw = keep.tile([P, DEGREES, PACK, MO], BF16)
        for l in range(DEGREES):
            nc.sync.dma_start(
                out=w_raw[:, l, :, :].rearrange("p t o -> p (t o)"),
                in_=weights[l].rearrange("(p t) o -> p (t o)", t=PACK),
            )

        x_words = x_raw[:].rearrange("p i c -> p (i c)").bitcast(F32)
        dummy = psum.tile([P, GROUP, MO], F32, name="bank")

        def warm(q):
            first = q * I_LOAD * C // 2
            nc.tensor.matmul(
                dummy[:, 0, :], lhsT=identity[:], rhs=x_words[:, first : first + P], start=True, stop=True
            )

        x_by_channel = keep.tile([P, C, 2, MI // 2], BF16)
        for q in range(LOADS):
            i_range = slice(q * I_LOAD, (q + 1) * I_LOAD)
            k_range = slice(q * I_LOAD // 2, (q + 1) * I_LOAD // 2)
            for a in [slice(0, 4)] if q < LOADS - 1 else [slice(a, a + 1) for a in range(4)]:
                nc.vector.tensor_copy(
                    out=x_by_channel[:, :, :, k_range].rearrange("p (a b) u k -> p a u k b", b=4)[:, a],
                    in_=x_raw[:, i_range, :].rearrange("p (k u) (a b) -> p a u k b", u=2, b=4)[:, a],
                )

        w_grouped = keep.tile([P, DEGREES, MO, PACK], BF16, align_bytes=64)
        for l in range(DEGREES):
            (nc.scalar.copy if l == 0 else nc.vector.tensor_copy)(
                out=w_grouped[:, l, :, :].rearrange("p (a b) (u e) -> p a u e b", b=4, u=2),
                in_=w_raw[:, l, :, :].rearrange("p (e u) (a b) -> p a u e b", b=4, u=2),
            )
        w_codes = keep.tile([P, DEGREES * MO], U32, align_bytes=64)
        w_scales = keep.tile([P, DEGREES * MO], U8, align_bytes=64)

        def quantise_weights(degrees):
            columns = slice(degrees.start * MO, degrees.stop * MO)
            nc.vector.quantize_mx(
                out=w_codes[:, columns].bitcast(FP8X4),
                scales=w_scales[:, columns],
                in_=w_grouped[:, degrees.start : degrees.stop].rearrange("p l o t -> p (l o t)"),
            )

        x_grouped = keep.tile([P, C, N * PACK], BF16, align_bytes=64)
        words = x_by_channel[:].bitcast(F32)
        x_grouped_words = x_grouped[:].bitcast(F32)
        x_codes = keep.tile([P, C * N], U32, align_bytes=64)
        x_scales = keep.tile([P, C * N], U8, align_bytes=64)
        result = keep.tile([P, MO, C], F32)

        def transpose(c_range):
            flipped = psum.tile([P, len(c_range), 2, N], F32, name="bank")
            for b, c in enumerate(c_range):
                for u in range(2):
                    nc.tensor.transpose(flipped[:, b, u, :], words[:, c, u, :], identity[:])
            return flipped

        def collect(engine_copy, c_range, flipped):
            engine_copy(
                out=x_grouped_words[:, c_range.start : c_range.stop, :].rearrange("p b (n u) -> p b n u", u=2),
                in_=flipped[:].rearrange("p b u n -> p b n u"),
            )

        def quantise(c_range):
            columns = slice(c_range.start * N, c_range.stop * N)
            nc.vector.quantize_mx(
                out=x_codes[:, columns].bitcast(FP8X4),
                scales=x_scales[:, columns],
                in_=x_grouped[:, c_range.start : c_range.stop, :].rearrange("p c m -> p (c m)"),
            )

        def multiply(g):
            acc = psum.tile([P, GROUP, MO], F32, name="bank")
            for b in range(GROUP):
                c = g * GROUP + b
                l = degree_of_channel[c]
                nc.tensor.matmul_mx(
                    out=acc[:, b, :],
                    lhsT=x_codes[:, c * N : (c + 1) * N].bitcast(FP8X4),
                    lhsT_scale=x_scales[:, c * N : (c + 1) * N],
                    rhs=w_codes[:, l * MO : (l + 1) * MO].bitcast(FP8X4),
                    rhs_scale=w_scales[:, l * MO : (l + 1) * MO],
                    start=True,
                    stop=True,
                )
            return acc

        def gather(engine_copy, g, o_range, acc):
            engine_copy(
                out=result[:, o_range, g * GROUP : (g + 1) * GROUP],
                in_=acc[:, :, o_range].rearrange("p b o -> p o b"),
            )

        with tc.manual_schedule():
            for q in WARM:
                warm(q)
            for_vector = []
            for i, count in enumerate(BANKS):
                c_range = range(sum(BANKS[:i]), sum(BANKS[:i]) + count)
                flipped = transpose(c_range)
                if i in VECTOR_BANKS:
                    for_vector.append((c_range, flipped))
                else:
                    collect(nc.scalar.copy, c_range, flipped)
                if i in WARM_BANKS:
                    warm(LOADS - 1)
            quantise_weights(range(0, 2))
            quantise_weights(range(2, 4))
            collect(nc.vector.tensor_copy, *for_vector[0])
            quantise(range(0, 4))
            quantise(range(4, 8))
            quantise(range(8, 12))
            quantise(range(12, 14))
            quantise(range(14, 16))
            acc = [multiply(g) for g in range(GROUPS)]
            low, high = slice(0, STORES[0]), slice(STORES[0], MO)

            def store(o_range):
                nc.sync.dma_start(
                    out=out[:, o_range, :].rearrange("n o c -> n (o c)"),
                    in_=result[:, o_range, :].rearrange("p o c -> p (o c)"),
                )

            gather(nc.scalar.copy, 0, low, acc[0])
            gather(nc.scalar.copy, 1, low, acc[1])
            gather(nc.scalar.copy, 0, high, acc[0])
            gather(nc.scalar.copy, 2, low, acc[2])
            gather(nc.vector.tensor_copy, 3, low, acc[3])
            store(low)
            gather(nc.scalar.copy, 1, high, acc[1])
            gather(nc.scalar.copy, 2, high, acc[2])
            gather(nc.vector.tensor_copy, 3, high, acc[3])
            store(high)
